import numpy as np
import ml_dtypes


def mxq(x, axis, fmt="e4m3"):
    dtype, down = {"e4m3": (ml_dtypes.float8_e4m3fn, 7), "e5m2": (ml_dtypes.float8_e5m2, 14)}[fmt]
    v = np.moveaxis(np.asarray(x, np.float32).astype(ml_dtypes.bfloat16).astype(np.float64), axis, -1)
    blocks = v.reshape(v.shape[:-1] + (-1, 32))
    amax = np.abs(blocks).max(-1, keepdims=True)
    byte = np.maximum(np.where(amax > 0, np.frexp(amax)[1] - 1 + 127, 0) - down, 1)
    scale = np.exp2(byte - 127.0)
    codes = (blocks / scale).astype(np.float32).astype(dtype).astype(np.float64)
    return np.moveaxis((codes * scale).reshape(v.shape), -1, axis)


WIDE = False


def mx_kscale(k):
    if not WIDE:
        return np.ones(k)
    levels = np.array([10, -10, 5, -5, 0])
    a = np.random.permutation(np.resize(levels, k // 512 * 4)).reshape(k // 512, 4)
    idx = np.arange(k)
    return np.exp2(a[idx // 512, idx % 128 // 32])


BF16 = ml_dtypes.bfloat16


def bf(x):
    return np.asarray(x, np.float32).astype(BF16)


def f64(x):
    return np.asarray(x).astype(np.float64)


B, S, D, H, DH = 2, 256, 2048, 16, 128
ROPE_BASE = 10000.0


def rope_tables():
    inv_freq = 1.0 / (ROPE_BASE ** (f64(np.arange(0, DH, 2)) / DH))
    freqs = f64(np.arange(S))[:, None] * inv_freq[None, :]
    return np.cos(freqs), np.sin(freqs)


def rope_interleaved(t, cos, sin):
    x1 = t[..., 0::2]
    x2 = t[..., 1::2]
    c = cos[None, :, None, :]
    s_ = sin[None, :, None, :]
    even = x1 * c - x2 * s_
    odd = x1 * s_ + x2 * c
    return np.stack((even, odd), axis=-1).reshape(t.shape)


def setup_inputs():
    s = mx_kscale(D)
    return {"x": bf(np.random.standard_normal((B, S, D)) * s),
            "wqk_w": bf(np.random.standard_normal((2 * H * DH, D)) / np.sqrt(D) / s[None, :])}


def reference(x, wqk_w):
    xqk = (mxq(f64(x), 2, "e4m3") @ mxq(f64(wqk_w), 1, "e4m3").T).reshape(B, S, 2, H, DH)
    cos, sin = rope_tables()
    q = rope_interleaved(xqk[:, :, 0], cos, sin).transpose(0, 2, 1, 3)
    k = rope_interleaved(xqk[:, :, 1], cos, sin).transpose(0, 2, 1, 3)
    return q, k

@@ -1,0 +1,228 @@
+import math
+from contextlib import ExitStack
+
+import concourse.mybir as mybir
+from concourse.masks import make_identity
+
+F32 = mybir.dt.float32
+BF16 = mybir.dt.bfloat16
+I32 = mybir.dt.int32
+U32 = mybir.dt.uint32
+U8 = mybir.dt.uint8
+FP8X4 = mybir.dt.float8_e4m3fn_x4
+ALU = mybir.AluOpType
+ACT = mybir.ActivationFunctionType
+
+P = 128
+BATCH, SEQ, D_MODEL, HEADS, D_HEAD = 2, 256, 2048, 16, 128
+ROPE_BASE = 10000.0
+PAIRS = D_HEAD // 2
+K_PASS = 4 * P
+PASSES = D_MODEL // K_PASS
+ROW_WORDS = D_MODEL // 2
+PASS_WORDS = K_PASS // 2
+BLOCKS = 4
+CHUNK = BLOCKS * P
+W_CHUNKS = 2 * HEADS * D_HEAD // CHUNK
+CHUNKS_PER_OUTPUT = W_CHUNKS // 2
+W_BUFS = 6
+ROUND_MAGIC = 1.5 * 2.0**23
+COS, SIN = 0, 1
+
+FLOPS = 2 * BATCH * SEQ * D_MODEL * 2 * HEADS * D_HEAD
+
+
+def build_rotation_tables(nc, consts):
+    position_int = consts.tile([P, 2], I32)
+    nc.gpsimd.iota(position_int[:], pattern=[[1, 2]], base=0, channel_multiplier=2)
+    position = consts.tile([P, 2], F32)
+    nc.vector.tensor_copy(out=position[:], in_=position_int[:])
+
+    freq = consts.tile([P, PAIRS], F32)
+    nc.vector.memset(freq[:, 0:1], 1.0)
+    width = 1
+    while width < PAIRS:
+        nc.vector.tensor_scalar_mul(
+            out=freq[:, width : 2 * width],
+            in0=freq[:, 0:width],
+            scalar1=ROPE_BASE ** (-width / PAIRS),
+        )
+        width *= 2
+
+    turns = consts.tile([P, 2, 2, PAIRS], F32)
+    for a in range(2):
+        nc.vector.tensor_scalar(
+            out=turns[:, a, SIN, :],
+            in0=freq[:],
+            scalar1=position[:, a : a + 1],
+            scalar2=1.0 / (2.0 * math.pi),
+            op0=ALU.mult,
+            op1=ALU.mult,
+        )
+    nc.vector.tensor_scalar_add(out=turns[:, :, COS, :], in0=turns[:, :, SIN, :], scalar1=0.25)
+
+    flat_turns = turns[:].rearrange("p a k i -> p (a k i)")
+    rounded = consts.tile([P, 4 * PAIRS], F32)
+    nc.vector.tensor_scalar_add(out=rounded[:], in0=flat_turns, scalar1=ROUND_MAGIC)
+    excess = consts.tile([P, 2, 2, PAIRS], F32)
+    nc.vector.scalar_tensor_tensor(
+        out=excess[:].rearrange("p a k i -> p (a k i)"),
+        in0=rounded[:],
+        scalar=ROUND_MAGIC,
+        in1=flat_turns,
+        op0=ALU.subtract,
+        op1=ALU.subtract,
+    )
+
+    from_even = consts.tile([P, 2, PAIRS, 2], F32)
+    nc.scalar.activation(
+        out=from_even[:],
+        in_=excess[:].rearrange("p a k i -> p a i k"),
+        func=ACT.Sin,
+        scale=-2.0 * math.pi,
+    )
+    from_odd = consts.tile([P, 2, PAIRS, 2], F32)
+    nc.scalar.activation(
+        out=from_odd[:, :, :, 0], in_=excess[:, :, SIN, :], func=ACT.Sin, scale=2.0 * math.pi
+    )
+    nc.scalar.activation(
+        out=from_odd[:, :, :, 1], in_=excess[:, :, COS, :], func=ACT.Sin, scale=-2.0 * math.pi
+    )
+    return from_even, from_odd
+
+
+def tile_attention_pa_kernel(tc, x, wqk_w, out_0, out_1):
+    nc = tc.nc
+    with ExitStack() as stack:
+        consts = stack.enter_context(tc.tile_pool(name="consts", bufs=1))
+        w_pool = stack.enter_context(tc.tile_pool(name="w_rows", bufs=W_BUFS))
+        grouped_pool = stack.enter_context(tc.tile_pool(name="grouped", bufs=4))
+        w_mx_pool = stack.enter_context(tc.tile_pool(name="w_mx", bufs=2))
+        rope_pool = stack.enter_context(tc.tile_pool(name="rope", bufs=3))
+        transposed_pool = stack.enter_context(tc.psum_pool(name="transposed", bufs=4))
+        sums_pool = stack.enter_context(tc.psum_pool(name="sums", bufs=4))
+        stack.enter_context(tc.manual_schedule())
+
+        def load_w_chunk(c):
+            w_rows = w_pool.tile([P, BLOCKS * D_MODEL], BF16)
+            nc.sync.dma_start(
+                out=w_rows[:].rearrange("p (r k) -> p r k", r=BLOCKS),
+                in_=wqk_w[c * CHUNK : (c + 1) * CHUNK, :].rearrange("(r p) k -> p r k", p=P),
+            )
+            return w_rows
+
+        def transpose_pass(rows, g):
+            row_words = rows[:].bitcast(F32)
+            grouped = grouped_pool.tile([P, 4 * CHUNK], BF16, align_bytes=64)
+            grouped_words = grouped[:].bitcast(F32).rearrange("p (r c u) -> p r c u", r=BLOCKS, u=2)
+            for first_block in range(0, BLOCKS, 2):
+                bank = transposed_pool.tile([P, 2, 2, P], F32)
+                for r in range(2):
+                    for u in range(2):
+                        start = (first_block + r) * ROW_WORDS + g * PASS_WORDS + u * P
+                        nc.tensor.transpose(
+                            bank[:, r, u, :], row_words[:, start : start + P], identity[:]
+                        )
+                nc.scalar.copy(
+                    out=grouped_words[:, first_block : first_block + 2, :, :],
+                    in_=bank[:].rearrange("p r u c -> p r c u"),
+                )
+            return grouped
+
+        def quantise_pass(grouped, codes, scales, g):
+            nc.vector.quantize_mx(
+                out=codes[:, g, :].bitcast(FP8X4), scales=scales[:, g, :], in_=grouped[:]
+            )
+
+        def project(token_tile, w_codes, w_scales):
+            tokens = slice(token_tile * P, (token_tile + 1) * P)
+            sums = sums_pool.tile([P, CHUNK], F32)
+            for g in range(PASSES):
+                nc.tensor.matmul_mx(
+                    out=sums[:],
+                    lhsT=x_codes[:, g, tokens].bitcast(FP8X4),
+                    lhsT_scale=x_scales[:, g, tokens],
+                    rhs=w_codes[:, g, :].bitcast(FP8X4),
+                    rhs_scale=w_scales[:, g, :],
+                    start=(g == 0),
+                    stop=(g == PASSES - 1),
+                )
+            return sums
+
+        def rotate(sums, a, rotated):
+            shape = [P, BLOCKS, PAIRS, 2]
+            pairs = sums[:].rearrange("p (h i e) -> p h i e", h=BLOCKS, e=2)
+            even_part = rope_pool.tile(shape, F32)
+            nc.vector.tensor_tensor(
+                out=even_part[:],
+                in0=pairs[:, :, :, 0:1].to_broadcast(shape),
+                in1=from_even[:, a, :, :].unsqueeze(1).to_broadcast(shape),
+                op=ALU.mult,
+            )
+            odd_part = rope_pool.tile(shape, F32)
+            nc.vector.tensor_tensor(
+                out=odd_part[:],
+                in0=pairs[:, :, :, 1:2].to_broadcast(shape),
+                in1=from_odd[:, a, :, :].unsqueeze(1).to_broadcast(shape),
+                op=ALU.mult,
+            )
+            nc.gpsimd.tensor_tensor(
+                out=rotated[:, :, a, :],
+                in0=even_part[:].rearrange("p h i e -> p h (i e)"),
+                in1=odd_part[:].rearrange("p h i e -> p h (i e)"),
+                op=ALU.add,
+            )
+
+        def store(rotated, c, b):
+            output = out_0 if c < CHUNKS_PER_OUTPUT else out_1
+            first_head = (c % CHUNKS_PER_OUTPUT) * BLOCKS
+            nc.sync.dma_start(
+                out=output[b, first_head : first_head + BLOCKS, :, :].rearrange(
+                    "h (m a) j -> m h (a j)", a=2
+                ),
+                in_=rotated[:].rearrange("p h a j -> p h (a j)"),
+            )
+
+        x_rows = consts.tile([P, BLOCKS * D_MODEL], BF16)
+        for b in range(BATCH):
+            nc.sync.dma_start(
+                out=x_rows[:, 2 * b * D_MODEL : 2 * (b + 1) * D_MODEL],
+                in_=x[b, :, :].rearrange("(m a) k -> m (a k)", a=2),
+            )
+        w_rows_of = {}
+        for c in range(W_BUFS):
+            w_rows_of[c] = load_w_chunk(c)
+
+        identity = consts.tile([P, P], F32)
+        make_identity(nc, identity[:])
+        from_even, from_odd = build_rotation_tables(nc, consts)
+
+        x_codes = consts.tile([P, PASSES, CHUNK], U32, align_bytes=64)
+        x_scales = consts.tile([P, PASSES, CHUNK], U8, align_bytes=64)
+        for g in range(PASSES):
+            quantise_pass(transpose_pass(x_rows, g), x_codes, x_scales, g)
+
+        w_codes = w_mx_pool.tile([P, PASSES, CHUNK], U32, align_bytes=64)
+        w_scales = w_mx_pool.tile([P, PASSES, CHUNK], U8, align_bytes=64)
+        for g in range(PASSES):
+            quantise_pass(transpose_pass(w_rows_of[0], g), w_codes, w_scales, g)
+
+        for c in range(W_CHUNKS):
+            if c + W_BUFS < W_CHUNKS:
+                w_rows_of[c + W_BUFS] = load_w_chunk(c + W_BUFS)
+            more = c + 1 < W_CHUNKS
+            if more:
+                next_codes = w_mx_pool.tile([P, PASSES, CHUNK], U32, align_bytes=64, tag="w_codes")
+                next_scales = w_mx_pool.tile([P, PASSES, CHUNK], U8, align_bytes=64, tag="w_scales")
+            for b in range(BATCH):
+                next_passes = (2 * b, 2 * b + 1) if more else ()
+                grouped_of = {g: transpose_pass(w_rows_of[c + 1], g) for g in next_passes}
+                sums_of = {a: project(2 * b + a, w_codes, w_scales) for a in range(2)}
+                for g in next_passes:
+                    quantise_pass(grouped_of[g], next_codes, next_scales, g)
+                rotated = rope_pool.tile([P, BLOCKS, 2, D_HEAD], F32)
+                for a in range(2):
+                    rotate(sums_of[a], a, rotated)
+                store(rotated, c, b)
+            if more:
+                w_codes, w_scales = next_codes, next_scales

@@ -74,21 +74,20 @@ def build_rotation_tables(nc, consts):
         op1=ALU.subtract,
     )
 
-    from_even = consts.tile([P, 2, PAIRS, 2], F32)
+    factors = consts.tile([P, 2, 2, PAIRS, 2], F32)
     nc.scalar.activation(
-        out=from_even[:],
+        out=factors[:, :, 0, :, :],
         in_=excess[:].rearrange("p a k i -> p a i k"),
         func=ACT.Sin,
         scale=-2.0 * math.pi,
     )
-    from_odd = consts.tile([P, 2, PAIRS, 2], F32)
     nc.scalar.activation(
-        out=from_odd[:, :, :, 0], in_=excess[:, :, SIN, :], func=ACT.Sin, scale=2.0 * math.pi
+        out=factors[:, :, 1, :, 0], in_=excess[:, :, SIN, :], func=ACT.Sin, scale=2.0 * math.pi
     )
     nc.scalar.activation(
-        out=from_odd[:, :, :, 1], in_=excess[:, :, COS, :], func=ACT.Sin, scale=-2.0 * math.pi
+        out=factors[:, :, 1, :, 1], in_=excess[:, :, COS, :], func=ACT.Sin, scale=-2.0 * math.pi
     )
-    return from_even, from_odd
+    return factors
 
 
 def tile_attention_pa_kernel(tc, x, wqk_w, out_0, out_1):
@@ -96,7 +95,7 @@ def tile_attention_pa_kernel(tc, x, wqk_w, out_0, out_1):
     with ExitStack() as stack:
         consts = stack.enter_context(tc.tile_pool(name="consts", bufs=1))
         w_pool = stack.enter_context(tc.tile_pool(name="w_rows", bufs=W_BUFS))
-        grouped_pool = stack.enter_context(tc.tile_pool(name="grouped", bufs=4))
+        grouped_pool = stack.enter_context(tc.tile_pool(name="grouped", bufs=3))
         w_mx_pool = stack.enter_context(tc.tile_pool(name="w_mx", bufs=2))
         rope_pool = stack.enter_context(tc.tile_pool(name="rope", bufs=3))
         transposed_pool = stack.enter_context(tc.psum_pool(name="transposed", bufs=4))
@@ -111,27 +110,35 @@ def tile_attention_pa_kernel(tc, x, wqk_w, out_0, out_1):
             )
             return w_rows
 
-        def transpose_pass(rows, g):
+        def transpose_two_passes(rows, first_pass):
             row_words = rows[:].bitcast(F32)
-            grouped = grouped_pool.tile([P, 4 * CHUNK], BF16, align_bytes=64)
-            grouped_words = grouped[:].bitcast(F32).rearrange("p (r c u) -> p r c u", r=BLOCKS, u=2)
-            for first_block in range(0, BLOCKS, 2):
-                bank = transposed_pool.tile([P, 2, 2, P], F32)
-                for r in range(2):
-                    for u in range(2):
-                        start = (first_block + r) * ROW_WORDS + g * PASS_WORDS + u * P
-                        nc.tensor.transpose(
-                            bank[:, r, u, :], row_words[:, start : start + P], identity[:]
-                        )
-                nc.scalar.copy(
-                    out=grouped_words[:, first_block : first_block + 2, :, :],
-                    in_=bank[:].rearrange("p r u c -> p r c u"),
-                )
+            grouped = grouped_pool.tile([P, 2 * 4 * CHUNK], BF16, align_bytes=64)
+            grouped_words = grouped[:].bitcast(F32).rearrange(
+                "p (g r c u) -> p g r c u", g=2, r=BLOCKS, u=2
+            )
+            for g in range(2):
+                for first_block in range(0, BLOCKS, 2):
+                    bank = transposed_pool.tile([P, 2, 2, P], F32)
+                    for r in range(2):
+                        for u in range(2):
+                            start = (
+                                (first_block + r) * ROW_WORDS + (first_pass + g) * PASS_WORDS + u * P
+                            )
+                            nc.tensor.transpose(
+                                bank[:, r, u, :], row_words[:, start : start + P], identity[:]
+                            )
+                    nc.scalar.copy(
+                        out=grouped_words[:, g, first_block : first_block + 2, :, :],
+                        in_=bank[:].rearrange("p r u c -> p r c u"),
+                    )
             return grouped
 
-        def quantise_pass(grouped, codes, scales, g):
+        def quantise_two_passes(grouped, codes, scales, first_pass):
+            passes = slice(first_pass, first_pass + 2)
             nc.vector.quantize_mx(
-                out=codes[:, g, :].bitcast(FP8X4), scales=scales[:, g, :], in_=grouped[:]
+                out=codes[:, passes, :].rearrange("p g n -> p (g n)").bitcast(FP8X4),
+                scales=scales[:, passes, :].rearrange("p g n -> p (g n)"),
+                in_=grouped[:],
             )
 
         def project(token_tile, w_codes, w_scales):
@@ -150,26 +157,21 @@ def tile_attention_pa_kernel(tc, x, wqk_w, out_0, out_1):
             return sums
 
         def rotate(sums, a, rotated):
-            shape = [P, BLOCKS, PAIRS, 2]
-            pairs = sums[:].rearrange("p (h i e) -> p h i e", h=BLOCKS, e=2)
-            even_part = rope_pool.tile(shape, F32)
+            shape = [P, 2, BLOCKS, PAIRS, 2]
+            products = rope_pool.tile(shape, F32)
             nc.vector.tensor_tensor(
-                out=even_part[:],
-                in0=pairs[:, :, :, 0:1].to_broadcast(shape),
-                in1=from_even[:, a, :, :].unsqueeze(1).to_broadcast(shape),
-                op=ALU.mult,
-            )
-            odd_part = rope_pool.tile(shape, F32)
-            nc.vector.tensor_tensor(
-                out=odd_part[:],
-                in0=pairs[:, :, :, 1:2].to_broadcast(shape),
-                in1=from_odd[:, a, :, :].unsqueeze(1).to_broadcast(shape),
+                out=products[:],
+                in0=sums[:]
+                .rearrange("p (h i k) -> p k h i", h=BLOCKS, k=2)
+                .unsqueeze(4)
+                .to_broadcast(shape),
+                in1=factors[:, a, :, :, :].unsqueeze(2).to_broadcast(shape),
                 op=ALU.mult,
             )
             nc.gpsimd.tensor_tensor(
                 out=rotated[:, :, a, :],
-                in0=even_part[:].rearrange("p h i e -> p h (i e)"),
-                in1=odd_part[:].rearrange("p h i e -> p h (i e)"),
+                in0=products[:, 0, :, :, :].rearrange("p h i e -> p h (i e)"),
+                in1=products[:, 1, :, :, :].rearrange("p h i e -> p h (i e)"),
                 op=ALU.add,
             )
 
@@ -195,17 +197,21 @@ def tile_attention_pa_kernel(tc, x, wqk_w, out_0, out_1):
 
         identity = consts.tile([P, P], F32)
         make_identity(nc, identity[:])
-        from_even, from_odd = build_rotation_tables(nc, consts)
+        factors = build_rotation_tables(nc, consts)
 
         x_codes = consts.tile([P, PASSES, CHUNK], U32, align_bytes=64)
         x_scales = consts.tile([P, PASSES, CHUNK], U8, align_bytes=64)
-        for g in range(PASSES):
-            quantise_pass(transpose_pass(x_rows, g), x_codes, x_scales, g)
+        for first_pass in range(0, PASSES, 2):
+            quantise_two_passes(
+                transpose_two_passes(x_rows, first_pass), x_codes, x_scales, first_pass
+            )
 
         w_codes = w_mx_pool.tile([P, PASSES, CHUNK], U32, align_bytes=64)
         w_scales = w_mx_pool.tile([P, PASSES, CHUNK], U8, align_bytes=64)
-        for g in range(PASSES):
-            quantise_pass(transpose_pass(w_rows_of[0], g), w_codes, w_scales, g)
+        for first_pass in range(0, PASSES, 2):
+            quantise_two_passes(
+                transpose_two_passes(w_rows_of[0], first_pass), w_codes, w_scales, first_pass
+            )
 
         for c in range(W_CHUNKS):
             if c + W_BUFS < W_CHUNKS:
@@ -215,11 +221,11 @@ def tile_attention_pa_kernel(tc, x, wqk_w, out_0, out_1):
                 next_codes = w_mx_pool.tile([P, PASSES, CHUNK], U32, align_bytes=64, tag="w_codes")
                 next_scales = w_mx_pool.tile([P, PASSES, CHUNK], U8, align_bytes=64, tag="w_scales")
             for b in range(BATCH):
-                next_passes = (2 * b, 2 * b + 1) if more else ()
-                grouped_of = {g: transpose_pass(w_rows_of[c + 1], g) for g in next_passes}
+                if more:
+                    grouped = transpose_two_passes(w_rows_of[c + 1], 2 * b)
                 sums_of = {a: project(2 * b + a, w_codes, w_scales) for a in range(2)}
-                for g in next_passes:
-                    quantise_pass(grouped_of[g], next_codes, next_scales, g)
+                if more:
+                    quantise_two_passes(grouped, next_codes, next_scales, 2 * b)
                 rotated = rope_pool.tile([P, BLOCKS, 2, D_HEAD], F32)
                 for a in range(2):
                     rotate(sums_of[a], a, rotated)

@@ -25,7 +25,10 @@ BLOCKS = 4
 CHUNK = BLOCKS * P
 W_CHUNKS = 2 * HEADS * D_HEAD // CHUNK
 CHUNKS_PER_OUTPUT = W_CHUNKS // 2
-W_BUFS = 6
+HALF_WORDS = ROW_WORDS // 2
+W_HALVES = 2 * W_CHUNKS
+W_BUFS = 10
+AHEAD = 2
 ROUND_MAGIC = 1.5 * 2.0**23
 COS, SIN = 0, 1
 
@@ -102,16 +105,18 @@ def tile_attention_pa_kernel(tc, x, wqk_w, out_0, out_1):
         sums_pool = stack.enter_context(tc.psum_pool(name="sums", bufs=4))
         stack.enter_context(tc.manual_schedule())
 
-        def load_w_chunk(c):
-            w_rows = w_pool.tile([P, BLOCKS * D_MODEL], BF16)
+        def load_w_half(j):
+            c, pass_pair = divmod(j, 2)
+            w_half = w_pool.tile([P, BLOCKS * 2 * K_PASS], BF16)
             nc.sync.dma_start(
-                out=w_rows[:].rearrange("p (r k) -> p r k", r=BLOCKS),
-                in_=wqk_w[c * CHUNK : (c + 1) * CHUNK, :].rearrange("(r p) k -> p r k", p=P),
+                out=w_half[:].rearrange("p (r k) -> p r k", r=BLOCKS),
+                in_=wqk_w[
+                    c * CHUNK : (c + 1) * CHUNK, pass_pair * 2 * K_PASS : (pass_pair + 1) * 2 * K_PASS
+                ].rearrange("(r p) k -> p r k", p=P),
             )
-            return w_rows
+            return w_half[:].bitcast(F32).rearrange("p (r w) -> p r w", r=BLOCKS)
 
-        def transpose_two_passes(rows, first_pass):
-            row_words = rows[:].bitcast(F32)
+        def transpose_two_passes(half_rows, vector_helps):
             grouped = grouped_pool.tile([P, 2 * 4 * CHUNK], BF16, align_bytes=64)
             grouped_words = grouped[:].bitcast(F32).rearrange(
                 "p (g r c u) -> p g r c u", g=2, r=BLOCKS, u=2
@@ -121,20 +126,22 @@ def tile_attention_pa_kernel(tc, x, wqk_w, out_0, out_1):
                     bank = transposed_pool.tile([P, 2, 2, P], F32)
                     for r in range(2):
                         for u in range(2):
-                            start = (
-                                (first_block + r) * ROW_WORDS + (first_pass + g) * PASS_WORDS + u * P
-                            )
+                            start = g * PASS_WORDS + u * P
                             nc.tensor.transpose(
-                                bank[:, r, u, :], row_words[:, start : start + P], identity[:]
+                                bank[:, r, u, :],
+                                half_rows[:, first_block + r, start : start + P],
+                                identity[:],
                             )
-                    nc.scalar.copy(
-                        out=grouped_words[:, g, first_block : first_block + 2, :, :],
-                        in_=bank[:].rearrange("p r u c -> p r c u"),
-                    )
+                    side_by_side = grouped_words[:, g, first_block : first_block + 2, :, :]
+                    by_column = bank[:].rearrange("p r u c -> p r c u")
+                    if vector_helps and first_block > 0:
+                        nc.vector.tensor_copy(out=side_by_side, in_=by_column)
+                    else:
+                        nc.scalar.copy(out=side_by_side, in_=by_column)
             return grouped
 
-        def quantise_two_passes(grouped, codes, scales, first_pass):
-            passes = slice(first_pass, first_pass + 2)
+        def quantise_two_passes(grouped, codes, scales, pass_pair):
+            passes = slice(2 * pass_pair, 2 * pass_pair + 2)
             nc.vector.quantize_mx(
                 out=codes[:, passes, :].rearrange("p g n -> p (g n)").bitcast(FP8X4),
                 scales=scales[:, passes, :].rearrange("p g n -> p (g n)"),
@@ -156,24 +163,27 @@ def tile_attention_pa_kernel(tc, x, wqk_w, out_0, out_1):
                 )
             return sums
 
-        def rotate(sums, a, rotated):
+        def rotate(sums_of):
             shape = [P, 2, BLOCKS, PAIRS, 2]
-            products = rope_pool.tile(shape, F32)
-            nc.vector.tensor_tensor(
-                out=products[:],
-                in0=sums[:]
-                .rearrange("p (h i k) -> p k h i", h=BLOCKS, k=2)
-                .unsqueeze(4)
-                .to_broadcast(shape),
-                in1=factors[:, a, :, :, :].unsqueeze(2).to_broadcast(shape),
-                op=ALU.mult,
-            )
+            products = rope_pool.tile([P, 2] + shape[1:], F32)
+            for a in range(2):
+                nc.vector.tensor_tensor(
+                    out=products[:, a, :, :, :, :],
+                    in0=sums_of[a][:]
+                    .rearrange("p (h i k) -> p k h i", h=BLOCKS, k=2)
+                    .unsqueeze(4)
+                    .to_broadcast(shape),
+                    in1=factors[:, a, :, :, :].unsqueeze(2).to_broadcast(shape),
+                    op=ALU.mult,
+                )
+            rotated = rope_pool.tile([P, BLOCKS, 2, D_HEAD], F32)
             nc.gpsimd.tensor_tensor(
-                out=rotated[:, :, a, :],
-                in0=products[:, 0, :, :, :].rearrange("p h i e -> p h (i e)"),
-                in1=products[:, 1, :, :, :].rearrange("p h i e -> p h (i e)"),
+                out=rotated[:],
+                in0=products[:, :, 0, :, :, :].rearrange("p a h i e -> p h a (i e)"),
+                in1=products[:, :, 1, :, :, :].rearrange("p a h i e -> p h a (i e)"),
                 op=ALU.add,
             )
+            return rotated
 
         def store(rotated, c, b):
             output = out_0 if c < CHUNKS_PER_OUTPUT else out_1
@@ -191,44 +201,42 @@ def tile_attention_pa_kernel(tc, x, wqk_w, out_0, out_1):
                 out=x_rows[:, 2 * b * D_MODEL : 2 * (b + 1) * D_MODEL],
                 in_=x[b, :, :].rearrange("(m a) k -> m (a k)", a=2),
             )
-        w_rows_of = {}
-        for c in range(W_BUFS):
-            w_rows_of[c] = load_w_chunk(c)
+        w_half_of = {j: load_w_half(j) for j in range(W_BUFS)}
 
         identity = consts.tile([P, P], F32)
         make_identity(nc, identity[:])
         factors = build_rotation_tables(nc, consts)
 
+        x_words = x_rows[:].bitcast(F32).rearrange("p (r w) -> p r w", r=BLOCKS)
         x_codes = consts.tile([P, PASSES, CHUNK], U32, align_bytes=64)
         x_scales = consts.tile([P, PASSES, CHUNK], U8, align_bytes=64)
-        for first_pass in range(0, PASSES, 2):
-            quantise_two_passes(
-                transpose_two_passes(x_rows, first_pass), x_codes, x_scales, first_pass
-            )
+        for pass_pair in range(2):
+            half_rows = x_words[:, :, pass_pair * HALF_WORDS : (pass_pair + 1) * HALF_WORDS]
+            grouped = transpose_two_passes(half_rows, vector_helps=True)
+            quantise_two_passes(grouped, x_codes, x_scales, pass_pair)
 
-        w_codes = w_mx_pool.tile([P, PASSES, CHUNK], U32, align_bytes=64)
-        w_scales = w_mx_pool.tile([P, PASSES, CHUNK], U8, align_bytes=64)
-        for first_pass in range(0, PASSES, 2):
-            quantise_two_passes(
-                transpose_two_passes(w_rows_of[0], first_pass), w_codes, w_scales, first_pass
-            )
+        w_mx_of = {}
 
-        for c in range(W_CHUNKS):
-            if c + W_BUFS < W_CHUNKS:
-                w_rows_of[c + W_BUFS] = load_w_chunk(c + W_BUFS)
-            more = c + 1 < W_CHUNKS
-            if more:
-                next_codes = w_mx_pool.tile([P, PASSES, CHUNK], U32, align_bytes=64, tag="w_codes")
-                next_scales = w_mx_pool.tile([P, PASSES, CHUNK], U8, align_bytes=64, tag="w_scales")
-            for b in range(BATCH):
-                if more:
-                    grouped = transpose_two_passes(w_rows_of[c + 1], 2 * b)
-                sums_of = {a: project(2 * b + a, w_codes, w_scales) for a in range(2)}
-                if more:
-                    quantise_two_passes(grouped, next_codes, next_scales, 2 * b)
-                rotated = rope_pool.tile([P, BLOCKS, 2, D_HEAD], F32)
-                for a in range(2):
-                    rotate(sums_of[a], a, rotated)
-                store(rotated, c, b)
-            if more:
-                w_codes, w_scales = next_codes, next_scales
+        def new_w_mx(c):
+            w_codes = w_mx_pool.tile([P, PASSES, CHUNK], U32, align_bytes=64)
+            w_scales = w_mx_pool.tile([P, PASSES, CHUNK], U8, align_bytes=64)
+            w_mx_of[c] = (w_codes, w_scales)
+
+        new_w_mx(0)
+        for j in range(AHEAD):
+            grouped = transpose_two_passes(w_half_of[j], vector_helps=True)
+            quantise_two_passes(grouped, w_mx_of[0][0], w_mx_of[0][1], j)
+
+        for k in range(W_HALVES):
+            c, b = divmod(k, 2)
+            if k + W_BUFS < W_HALVES:
+                w_half_of[k + W_BUFS] = load_w_half(k + W_BUFS)
+            j = k + AHEAD
+            if j < W_HALVES:
+                if j % 2 == 0:
+                    new_w_mx(j // 2)
+                grouped = transpose_two_passes(w_half_of[j], vector_helps=False)
+            sums_of = {a: project(2 * b + a, w_mx_of[c][0], w_mx_of[c][1]) for a in range(2)}
+            if j < W_HALVES:
+                quantise_two_passes(grouped, w_mx_of[j // 2][0], w_mx_of[j // 2][1], j % 2)
+            store(rotate(sums_of), c, b)

@@ -27,7 +27,8 @@ W_CHUNKS = 2 * HEADS * D_HEAD // CHUNK
 CHUNKS_PER_OUTPUT = W_CHUNKS // 2
 HALF_WORDS = ROW_WORDS // 2
 W_HALVES = 2 * W_CHUNKS
-W_BUFS = 10
+LOADS_AHEAD = 6
+W_BUFS = LOADS_AHEAD + 2
 AHEAD = 2
 ROUND_MAGIC = 1.5 * 2.0**23
 COS, SIN = 0, 1
@@ -108,13 +109,13 @@ def tile_attention_pa_kernel(tc, x, wqk_w, out_0, out_1):
         def load_w_half(j):
             c, pass_pair = divmod(j, 2)
             w_half = w_pool.tile([P, BLOCKS * 2 * K_PASS], BF16)
-            nc.sync.dma_start(
+            nc.scalar.dma_start(
                 out=w_half[:].rearrange("p (r k) -> p r k", r=BLOCKS),
                 in_=wqk_w[
                     c * CHUNK : (c + 1) * CHUNK, pass_pair * 2 * K_PASS : (pass_pair + 1) * 2 * K_PASS
                 ].rearrange("(r p) k -> p r k", p=P),
             )
-            return w_half[:].bitcast(F32).rearrange("p (r w) -> p r w", r=BLOCKS)
+            w_half_of[j] = w_half[:].bitcast(F32).rearrange("p (r w) -> p r w", r=BLOCKS)
 
         def transpose_two_passes(half_rows, vector_helps):
             grouped = grouped_pool.tile([P, 2 * 4 * CHUNK], BF16, align_bytes=64)
@@ -197,11 +198,13 @@ def tile_attention_pa_kernel(tc, x, wqk_w, out_0, out_1):
 
         x_rows = consts.tile([P, BLOCKS * D_MODEL], BF16)
         for b in range(BATCH):
-            nc.sync.dma_start(
+            nc.scalar.dma_start(
                 out=x_rows[:, 2 * b * D_MODEL : 2 * (b + 1) * D_MODEL],
                 in_=x[b, :, :].rearrange("(m a) k -> m (a k)", a=2),
             )
-        w_half_of = {j: load_w_half(j) for j in range(W_BUFS)}
+        w_half_of = {}
+        for j in range(LOADS_AHEAD):
+            load_w_half(j)
 
         identity = consts.tile([P, P], F32)
         make_identity(nc, identity[:])
@@ -225,17 +228,18 @@ def tile_attention_pa_kernel(tc, x, wqk_w, out_0, out_1):
         new_w_mx(0)
         for j in range(AHEAD):
             grouped = transpose_two_passes(w_half_of[j], vector_helps=True)
+            load_w_half(j + LOADS_AHEAD)
             quantise_two_passes(grouped, w_mx_of[0][0], w_mx_of[0][1], j)
 
         for k in range(W_HALVES):
             c, b = divmod(k, 2)
-            if k + W_BUFS < W_HALVES:
-                w_half_of[k + W_BUFS] = load_w_half(k + W_BUFS)
             j = k + AHEAD
             if j < W_HALVES:
                 if j % 2 == 0:
                     new_w_mx(j // 2)
                 grouped = transpose_two_passes(w_half_of[j], vector_helps=False)
+            if j + LOADS_AHEAD < W_HALVES:
+                load_w_half(j + LOADS_AHEAD)
             sums_of = {a: project(2 * b + a, w_mx_of[c][0], w_mx_of[c][1]) for a in range(2)}
             if j < W_HALVES:
                 quantise_two_passes(grouped, w_mx_of[j // 2][0], w_mx_of[j // 2][1], j % 2)

@@ -27,8 +27,7 @@ W_CHUNKS = 2 * HEADS * D_HEAD // CHUNK
 CHUNKS_PER_OUTPUT = W_CHUNKS // 2
 HALF_WORDS = ROW_WORDS // 2
 W_HALVES = 2 * W_CHUNKS
-LOADS_AHEAD = 6
-W_BUFS = LOADS_AHEAD + 2
+W_BUFS = 10
 AHEAD = 2
 ROUND_MAGIC = 1.5 * 2.0**23
 COS, SIN = 0, 1
@@ -101,7 +100,7 @@ def tile_attention_pa_kernel(tc, x, wqk_w, out_0, out_1):
         w_pool = stack.enter_context(tc.tile_pool(name="w_rows", bufs=W_BUFS))
         grouped_pool = stack.enter_context(tc.tile_pool(name="grouped", bufs=3))
         w_mx_pool = stack.enter_context(tc.tile_pool(name="w_mx", bufs=2))
-        rope_pool = stack.enter_context(tc.tile_pool(name="rope", bufs=3))
+        rope_pool = stack.enter_context(tc.tile_pool(name="rope", bufs=4))
         transposed_pool = stack.enter_context(tc.psum_pool(name="transposed", bufs=4))
         sums_pool = stack.enter_context(tc.psum_pool(name="sums", bufs=4))
         stack.enter_context(tc.manual_schedule())
@@ -109,13 +108,13 @@ def tile_attention_pa_kernel(tc, x, wqk_w, out_0, out_1):
         def load_w_half(j):
             c, pass_pair = divmod(j, 2)
             w_half = w_pool.tile([P, BLOCKS * 2 * K_PASS], BF16)
-            nc.scalar.dma_start(
+            nc.sync.dma_start(
                 out=w_half[:].rearrange("p (r k) -> p r k", r=BLOCKS),
                 in_=wqk_w[
                     c * CHUNK : (c + 1) * CHUNK, pass_pair * 2 * K_PASS : (pass_pair + 1) * 2 * K_PASS
                 ].rearrange("(r p) k -> p r k", p=P),
             )
-            w_half_of[j] = w_half[:].bitcast(F32).rearrange("p (r w) -> p r w", r=BLOCKS)
+            return w_half[:].bitcast(F32).rearrange("p (r w) -> p r w", r=BLOCKS)
 
         def transpose_two_passes(half_rows, vector_helps):
             grouped = grouped_pool.tile([P, 2 * 4 * CHUNK], BF16, align_bytes=64)
@@ -164,27 +163,24 @@ def tile_attention_pa_kernel(tc, x, wqk_w, out_0, out_1):
                 )
             return sums
 
-        def rotate(sums_of):
+        def rotate(sums, a, rotated):
             shape = [P, 2, BLOCKS, PAIRS, 2]
-            products = rope_pool.tile([P, 2] + shape[1:], F32)
-            for a in range(2):
-                nc.vector.tensor_tensor(
-                    out=products[:, a, :, :, :, :],
-                    in0=sums_of[a][:]
-                    .rearrange("p (h i k) -> p k h i", h=BLOCKS, k=2)
-                    .unsqueeze(4)
-                    .to_broadcast(shape),
-                    in1=factors[:, a, :, :, :].unsqueeze(2).to_broadcast(shape),
-                    op=ALU.mult,
-                )
-            rotated = rope_pool.tile([P, BLOCKS, 2, D_HEAD], F32)
+            products = rope_pool.tile(shape, F32)
+            nc.vector.tensor_tensor(
+                out=products[:],
+                in0=sums[:]
+                .rearrange("p (h i k) -> p k h i", h=BLOCKS, k=2)
+                .unsqueeze(4)
+                .to_broadcast(shape),
+                in1=factors[:, a, :, :, :].unsqueeze(2).to_broadcast(shape),
+                op=ALU.mult,
+            )
             nc.gpsimd.tensor_tensor(
-                out=rotated[:],
-                in0=products[:, :, 0, :, :, :].rearrange("p a h i e -> p h a (i e)"),
-                in1=products[:, :, 1, :, :, :].rearrange("p a h i e -> p h a (i e)"),
+                out=rotated[:, :, a, :],
+                in0=products[:, 0, :, :, :].rearrange("p h i e -> p h (i e)"),
+                in1=products[:, 1, :, :, :].rearrange("p h i e -> p h (i e)"),
                 op=ALU.add,
             )
-            return rotated
 
         def store(rotated, c, b):
             output = out_0 if c < CHUNKS_PER_OUTPUT else out_1
@@ -198,13 +194,11 @@ def tile_attention_pa_kernel(tc, x, wqk_w, out_0, out_1):
 
         x_rows = consts.tile([P, BLOCKS * D_MODEL], BF16)
         for b in range(BATCH):
-            nc.scalar.dma_start(
+            nc.sync.dma_start(
                 out=x_rows[:, 2 * b * D_MODEL : 2 * (b + 1) * D_MODEL],
                 in_=x[b, :, :].rearrange("(m a) k -> m (a k)", a=2),
             )
-        w_half_of = {}
-        for j in range(LOADS_AHEAD):
-            load_w_half(j)
+        w_half_of = {j: load_w_half(j) for j in range(W_BUFS)}
 
         identity = consts.tile([P, P], F32)
         make_identity(nc, identity[:])
@@ -228,19 +222,21 @@ def tile_attention_pa_kernel(tc, x, wqk_w, out_0, out_1):
         new_w_mx(0)
         for j in range(AHEAD):
             grouped = transpose_two_passes(w_half_of[j], vector_helps=True)
-            load_w_half(j + LOADS_AHEAD)
             quantise_two_passes(grouped, w_mx_of[0][0], w_mx_of[0][1], j)
 
         for k in range(W_HALVES):
             c, b = divmod(k, 2)
+            if k + W_BUFS < W_HALVES:
+                w_half_of[k + W_BUFS] = load_w_half(k + W_BUFS)
             j = k + AHEAD
             if j < W_HALVES:
                 if j % 2 == 0:
                     new_w_mx(j // 2)
                 grouped = transpose_two_passes(w_half_of[j], vector_helps=False)
-            if j + LOADS_AHEAD < W_HALVES:
-                load_w_half(j + LOADS_AHEAD)
             sums_of = {a: project(2 * b + a, w_mx_of[c][0], w_mx_of[c][1]) for a in range(2)}
+            rotated = rope_pool.tile([P, BLOCKS, 2, D_HEAD], F32)
+            rotate(sums_of[0], 0, rotated)
             if j < W_HALVES:
                 quantise_two_passes(grouped, w_mx_of[j // 2][0], w_mx_of[j // 2][1], j % 2)
-            store(rotate(sums_of), c, b)
+            rotate(sums_of[1], 1, rotated)
+            store(rotated, c, b)

import math
from contextlib import ExitStack

import concourse.mybir as mybir
from concourse.masks import make_identity

F32 = mybir.dt.float32
BF16 = mybir.dt.bfloat16
I32 = mybir.dt.int32
U32 = mybir.dt.uint32
U8 = mybir.dt.uint8
FP8X4 = mybir.dt.float8_e4m3fn_x4
ALU = mybir.AluOpType
ACT = mybir.ActivationFunctionType

P = 128
BATCH, SEQ, D_MODEL, HEADS, D_HEAD = 2, 256, 2048, 16, 128
ROPE_BASE = 10000.0
PAIRS = D_HEAD // 2
K_PASS = 4 * P
PASSES = D_MODEL // K_PASS
ROW_WORDS = D_MODEL // 2
PASS_WORDS = K_PASS // 2
BLOCKS = 4
CHUNK = BLOCKS * P
W_CHUNKS = 2 * HEADS * D_HEAD // CHUNK
CHUNKS_PER_OUTPUT = W_CHUNKS // 2
HALF_WORDS = ROW_WORDS // 2
W_HALVES = 2 * W_CHUNKS
W_BUFS = 10
AHEAD = 2
ROUND_MAGIC = 1.5 * 2.0**23
COS, SIN = 0, 1

FLOPS = 2 * BATCH * SEQ * D_MODEL * 2 * HEADS * D_HEAD


def build_rotation_tables(nc, consts):
    position_int = consts.tile([P, 2], I32)
    nc.gpsimd.iota(position_int[:], pattern=[[1, 2]], base=0, channel_multiplier=2)
    position = consts.tile([P, 2], F32)
    nc.vector.tensor_copy(out=position[:], in_=position_int[:])

    freq = consts.tile([P, PAIRS], F32)
    nc.vector.memset(freq[:, 0:1], 1.0)
    width = 1
    while width < PAIRS:
        nc.vector.tensor_scalar_mul(
            out=freq[:, width : 2 * width],
            in0=freq[:, 0:width],
            scalar1=ROPE_BASE ** (-width / PAIRS),
        )
        width *= 2

    turns = consts.tile([P, 2, 2, PAIRS], F32)
    for a in range(2):
        nc.vector.tensor_scalar(
            out=turns[:, a, SIN, :],
            in0=freq[:],
            scalar1=position[:, a : a + 1],
            scalar2=1.0 / (2.0 * math.pi),
            op0=ALU.mult,
            op1=ALU.mult,
        )
    nc.vector.tensor_scalar_add(out=turns[:, :, COS, :], in0=turns[:, :, SIN, :], scalar1=0.25)

    flat_turns = turns[:].rearrange("p a k i -> p (a k i)")
    rounded = consts.tile([P, 4 * PAIRS], F32)
    nc.vector.tensor_scalar_add(out=rounded[:], in0=flat_turns, scalar1=ROUND_MAGIC)
    excess = consts.tile([P, 2, 2, PAIRS], F32)
    nc.vector.scalar_tensor_tensor(
        out=excess[:].rearrange("p a k i -> p (a k i)"),
        in0=rounded[:],
        scalar=ROUND_MAGIC,
        in1=flat_turns,
        op0=ALU.subtract,
        op1=ALU.subtract,
    )

    factors = consts.tile([P, 2, 2, PAIRS, 2], F32)
    nc.scalar.activation(
        out=factors[:, :, 0, :, :],
        in_=excess[:].rearrange("p a k i -> p a i k"),
        func=ACT.Sin,
        scale=-2.0 * math.pi,
    )
    nc.scalar.activation(
        out=factors[:, :, 1, :, 0], in_=excess[:, :, SIN, :], func=ACT.Sin, scale=2.0 * math.pi
    )
    nc.scalar.activation(
        out=factors[:, :, 1, :, 1], in_=excess[:, :, COS, :], func=ACT.Sin, scale=-2.0 * math.pi
    )
    return factors


def tile_attention_pa_kernel(tc, x, wqk_w, out_0, out_1):
    nc = tc.nc
    with ExitStack() as stack:
        consts = stack.enter_context(tc.tile_pool(name="consts", bufs=1))
        w_pool = stack.enter_context(tc.tile_pool(name="w_rows", bufs=W_BUFS))
        grouped_pool = stack.enter_context(tc.tile_pool(name="grouped", bufs=3))
        w_mx_pool = stack.enter_context(tc.tile_pool(name="w_mx", bufs=2))
        rope_pool = stack.enter_context(tc.tile_pool(name="rope", bufs=4))
        transposed_pool = stack.enter_context(tc.psum_pool(name="transposed", bufs=4))
        sums_pool = stack.enter_context(tc.psum_pool(name="sums", bufs=4))
        stack.enter_context(tc.manual_schedule())

        def load_w_half(j):
            c, pass_pair = divmod(j, 2)
            w_half = w_pool.tile([P, BLOCKS * 2 * K_PASS], BF16)
            nc.sync.dma_start(
                out=w_half[:].rearrange("p (r k) -> p r k", r=BLOCKS),
                in_=wqk_w[
                    c * CHUNK : (c + 1) * CHUNK, pass_pair * 2 * K_PASS : (pass_pair + 1) * 2 * K_PASS
                ].rearrange("(r p) k -> p r k", p=P),
            )
            return w_half[:].bitcast(F32).rearrange("p (r w) -> p r w", r=BLOCKS)

        def transpose_two_passes(half_rows, vector_helps):
            grouped = grouped_pool.tile([P, 2 * 4 * CHUNK], BF16, align_bytes=64)
            grouped_words = grouped[:].bitcast(F32).rearrange(
                "p (g r c u) -> p g r c u", g=2, r=BLOCKS, u=2
            )
            for g in range(2):
                for first_block in range(0, BLOCKS, 2):
                    bank = transposed_pool.tile([P, 2, 2, P], F32)
                    for r in range(2):
                        for u in range(2):
                            start = g * PASS_WORDS + u * P
                            nc.tensor.transpose(
                                bank[:, r, u, :],
                                half_rows[:, first_block + r, start : start + P],
                                identity[:],
                            )
                    side_by_side = grouped_words[:, g, first_block : first_block + 2, :, :]
                    by_column = bank[:].rearrange("p r u c -> p r c u")
                    if vector_helps and first_block > 0:
                        nc.vector.tensor_copy(out=side_by_side, in_=by_column)
                    else:
                        nc.scalar.copy(out=side_by_side, in_=by_column)
            return grouped

        def quantise_two_passes(grouped, codes, scales, pass_pair):
            passes = slice(2 * pass_pair, 2 * pass_pair + 2)
            nc.vector.quantize_mx(
                out=codes[:, passes, :].rearrange("p g n -> p (g n)").bitcast(FP8X4),
                scales=scales[:, passes, :].rearrange("p g n -> p (g n)"),
                in_=grouped[:],
            )

        def project(token_tile, w_codes, w_scales):
            tokens = slice(token_tile * P, (token_tile + 1) * P)
            sums = sums_pool.tile([P, CHUNK], F32)
            for g in range(PASSES):
                nc.tensor.matmul_mx(
                    out=sums[:],
                    lhsT=x_codes[:, g, tokens].bitcast(FP8X4),
                    lhsT_scale=x_scales[:, g, tokens],
                    rhs=w_codes[:, g, :].bitcast(FP8X4),
                    rhs_scale=w_scales[:, g, :],
                    start=(g == 0),
                    stop=(g == PASSES - 1),
                )
            return sums

        def rotate(sums, a, rotated):
            shape = [P, 2, BLOCKS, PAIRS, 2]
            products = rope_pool.tile(shape, F32)
            nc.vector.tensor_tensor(
                out=products[:],
                in0=sums[:]
                .rearrange("p (h i k) -> p k h i", h=BLOCKS, k=2)
                .unsqueeze(4)
                .to_broadcast(shape),
                in1=factors[:, a, :, :, :].unsqueeze(2).to_broadcast(shape),
                op=ALU.mult,
            )
            nc.gpsimd.tensor_tensor(
                out=rotated[:, :, a, :],
                in0=products[:, 0, :, :, :].rearrange("p h i e -> p h (i e)"),
                in1=products[:, 1, :, :, :].rearrange("p h i e -> p h (i e)"),
                op=ALU.add,
            )

        def store(rotated, c, b):
            output = out_0 if c < CHUNKS_PER_OUTPUT else out_1
            first_head = (c % CHUNKS_PER_OUTPUT) * BLOCKS
            nc.sync.dma_start(
                out=output[b, first_head : first_head + BLOCKS, :, :].rearrange(
                    "h (m a) j -> m h (a j)", a=2
                ),
                in_=rotated[:].rearrange("p h a j -> p h (a j)"),
            )

        x_rows = consts.tile([P, BLOCKS * D_MODEL], BF16)
        for b in range(BATCH):
            nc.sync.dma_start(
                out=x_rows[:, 2 * b * D_MODEL : 2 * (b + 1) * D_MODEL],
                in_=x[b, :, :].rearrange("(m a) k -> m (a k)", a=2),
            )
        w_half_of = {j: load_w_half(j) for j in range(W_BUFS)}

        identity = consts.tile([P, P], F32)
        make_identity(nc, identity[:])
        factors = build_rotation_tables(nc, consts)

        x_words = x_rows[:].bitcast(F32).rearrange("p (r w) -> p r w", r=BLOCKS)
        x_codes = consts.tile([P, PASSES, CHUNK], U32, align_bytes=64)
        x_scales = consts.tile([P, PASSES, CHUNK], U8, align_bytes=64)
        for pass_pair in range(2):
            half_rows = x_words[:, :, pass_pair * HALF_WORDS : (pass_pair + 1) * HALF_WORDS]
            grouped = transpose_two_passes(half_rows, vector_helps=True)
            quantise_two_passes(grouped, x_codes, x_scales, pass_pair)

        w_mx_of = {}

        def new_w_mx(c):
            w_codes = w_mx_pool.tile([P, PASSES, CHUNK], U32, align_bytes=64)
            w_scales = w_mx_pool.tile([P, PASSES, CHUNK], U8, align_bytes=64)
            w_mx_of[c] = (w_codes, w_scales)

        new_w_mx(0)
        for j in range(AHEAD):
            grouped = transpose_two_passes(w_half_of[j], vector_helps=True)
            quantise_two_passes(grouped, w_mx_of[0][0], w_mx_of[0][1], j)

        for k in range(W_HALVES):
            c, b = divmod(k, 2)
            if k + W_BUFS < W_HALVES:
                w_half_of[k + W_BUFS] = load_w_half(k + W_BUFS)
            j = k + AHEAD
            if j < W_HALVES:
                if j % 2 == 0:
                    new_w_mx(j // 2)
                grouped = transpose_two_passes(w_half_of[j], vector_helps=False)
            sums_of = {a: project(2 * b + a, w_mx_of[c][0], w_mx_of[c][1]) for a in range(2)}
            rotated = rope_pool.tile([P, BLOCKS, 2, D_HEAD], F32)
            rotate(sums_of[0], 0, rotated)
            if j < W_HALVES:
                quantise_two_passes(grouped, w_mx_of[j // 2][0], w_mx_of[j // 2][1], j % 2)
            rotate(sums_of[1], 1, rotated)
            store(rotated, c, b)
